import numpy as np
import ml_dtypes


def mxq(x, axis, fmt="e4m3"):
    dtype, down = {"e4m3": (ml_dtypes.float8_e4m3fn, 7), "e5m2": (ml_dtypes.float8_e5m2, 14)}[fmt]
    v = np.moveaxis(np.asarray(x, np.float32).astype(ml_dtypes.bfloat16).astype(np.float64), axis, -1)
    blocks = v.reshape(v.shape[:-1] + (-1, 32))
    amax = np.abs(blocks).max(-1, keepdims=True)
    byte = np.maximum(np.where(amax > 0, np.frexp(amax)[1] - 1 + 127, 0) - down, 1)
    scale = np.exp2(byte - 127.0)
    codes = (blocks / scale).astype(np.float32).astype(dtype).astype(np.float64)
    return np.moveaxis((codes * scale).reshape(v.shape), -1, axis)


WIDE = False


def mx_kscale(k):
    if not WIDE:
        return np.ones(k)
    levels = np.array([10, -10, 5, -5, 0])
    a = np.random.permutation(np.resize(levels, k // 512 * 4)).reshape(k // 512, 4)
    idx = np.arange(k)
    return np.exp2(a[idx // 512, idx % 128 // 32])


BF16 = ml_dtypes.bfloat16


def bf(x):
    return np.asarray(x, np.float32).astype(BF16)


def f64(x):
    return np.asarray(x).astype(np.float64)


B, S, D, N, A, F = 64, 64, 1024, 128, 128, 1024


def setup_inputs():
    s, t, u = mx_kscale(D), mx_kscale(F), mx_kscale(F)
    return {
        "slots": bf(np.random.standard_normal((B, S, D)) * s),
        "ident": bf(np.random.standard_normal((N, F)) * t),
        "Wq": bf(np.random.standard_normal((F, D)) / np.sqrt(D) / s[None, :] * u[:, None]),
        "Wk": bf(np.random.standard_normal((F, F)) * 2.0 / np.sqrt(F) / t[None, :] / u[:, None]),
    }


def reference(slots, ident, Wq, Wk):
    q = mxq(f64(slots), 2, "e4m3") @ mxq(f64(Wq), 1, "e4m3").T
    k = mxq(f64(ident), 1, "e4m3") @ mxq(f64(Wk), 1, "e4m3").T
    logits = D ** (-0.5) * (mxq(k, 1, "e4m3") @ mxq(q, 2, "e4m3").transpose(0, 2, 1))
    e = np.exp(logits - logits.max(-1, keepdims=True))
    return e / e.sum(-1, keepdims=True)

@@ -1,0 +1,262 @@
+from contextlib import ExitStack
+
+import concourse.mybir as mybir
+from concourse.masks import make_identity
+
+F32 = mybir.dt.float32
+BF16 = mybir.dt.bfloat16
+U32 = mybir.dt.uint32
+U8 = mybir.dt.uint8
+FP8X4 = mybir.dt.float8_e4m3fn_x4
+
+P = 128
+PACK = 4
+K_PASS = P * PACK
+
+SAMPLES, SLOTS, OBJECTS, FEATURES = 64, 64, 128, 1024
+PASSES = FEATURES // K_PASS
+PAIRS = PACK // 2
+BLOCK_COLS = PASSES * P * PACK
+GROUP = 4
+CHUNK_ROWS = GROUP * P
+CHUNKS = SAMPLES * SLOTS // CHUNK_ROWS
+CHUNK_SAMPLES = CHUNK_ROWS // SLOTS
+SCALE = FEATURES ** -0.5
+
+FLOPS = 2 * FEATURES * (SAMPLES * SLOTS * FEATURES + OBJECTS * FEATURES + SAMPLES * SLOTS * OBJECTS)
+
+
+def tile_actionbindingattention_pb_t_kernel(tc, slots, ident, Wq, Wk, out):
+    nc = tc.nc
+    slot_rows = slots.rearrange("b s d -> (b s) d")
+
+    with ExitStack() as ctx:
+        keep = ctx.enter_context(tc.tile_pool(name="keep", bufs=1))
+        stage = ctx.enter_context(tc.tile_pool(name="stage", bufs=2))
+        psum_t = ctx.enter_context(tc.psum_pool(name="psum_t", bufs=GROUP))
+        psum_p = ctx.enter_context(tc.psum_pool(name="psum_p", bufs=3))
+        psum_l = ctx.enter_context(tc.psum_pool(name="psum_l", bufs=1))
+        ctx.enter_context(tc.manual_schedule())
+
+        identity = keep.tile([P, P], F32)
+        make_identity(nc, identity[:])
+        warm = keep.tile([P, 1], F32)
+        nc.vector.memset(warm[:], 0.0)
+        nc.scalar.activation(out=warm[:], in_=warm[:], func=mybir.ActivationFunctionType.Exp)
+
+        def load_chunk(c):
+            rows = keep.tile([P, GROUP, FEATURES], BF16, name="x_raw%d" % c)
+            nc.sync.dma_start(
+                out=rows[:],
+                in_=slot_rows[c * CHUNK_ROWS : (c + 1) * CHUNK_ROWS, :].rearrange("(j p) d -> p j d", p=P),
+            )
+            return rows
+
+        def load_weight_half(w, h, name):
+            rows = keep.tile([P, PACK, FEATURES], BF16, name="%s_raw%d" % (name, h))
+            nc.sync.dma_start(
+                out=rows[:],
+                in_=w[h * K_PASS : (h + 1) * K_PASS, :].rearrange("(p t) d -> p t d", t=PACK),
+            )
+            return rows
+
+        x_raw = {}
+        x_raw[0] = load_chunk(0)
+        wq_raw = [load_weight_half(Wq, h, "wq") for h in range(PASSES)]
+        x_raw[1] = load_chunk(1)
+        ident_raw = keep.tile([P, 1, FEATURES], BF16)
+        nc.sync.dma_start(out=ident_raw[:, 0, :], in_=ident)
+        wk_raw = [load_weight_half(Wk, h, "wk") for h in range(PASSES)]
+        for c in range(2, CHUNKS):
+            x_raw[c] = load_chunk(c)
+
+        def transpose_blocks(rows):
+            banks = []
+            for j in range(rows.shape[1]):
+                words = rows[:, j, :].bitcast(F32)
+                bank = psum_t.tile([P, PASSES, PAIRS, P], F32)
+                for g in range(PASSES):
+                    for u in range(PAIRS):
+                        first = (g * PAIRS + u) * P
+                        nc.tensor.transpose(bank[:, g, u, :], words[:, first : first + P], identity[:])
+                banks.append(bank)
+            return banks
+
+        def regroup_blocks(banks, copies):
+            grouped = stage.tile([P, GROUP, BLOCK_COLS], BF16, align_bytes=64)
+            for j, bank in enumerate(banks):
+                copies[j % len(copies)](
+                    out=grouped[:, j, :].bitcast(F32).rearrange("p (g r u) -> p g r u", g=PASSES, u=PAIRS),
+                    in_=bank[:].rearrange("p g u r -> p g r u"),
+                )
+            return grouped[:, 0 : len(banks), :]
+
+        def quantise_blocks(grouped, codes, scales):
+            nc.vector.quantize_mx(
+                out=codes.rearrange("p j g r -> p (j g r)").bitcast(FP8X4),
+                scales=scales.rearrange("p j g r -> p (j g r)"),
+                in_=grouped.rearrange("p j k -> p (j k)"),
+            )
+
+        both = (nc.vector.tensor_copy, nc.scalar.copy)
+        vector_only = (nc.vector.tensor_copy,)
+
+        def prepare(rows, codes, scales):
+            quantise_blocks(regroup_blocks(transpose_blocks(rows), both), codes, scales)
+
+        x_grouped, x_codes, x_scales = {}, {}, {}
+
+        def new_chunk_codes(c):
+            codes = stage.tile([P, GROUP, PASSES, P], U32, name="x_codes", align_bytes=64)
+            scales = stage.tile([P, GROUP, PASSES, P], U8, name="x_scales", align_bytes=64)
+            x_codes[c], x_scales[c] = codes, scales
+
+        def quantise_chunk(c):
+            new_chunk_codes(c)
+            quantise_blocks(x_grouped[c], x_codes[c][:], x_scales[c][:])
+
+        def project(w_codes, w_scales, h, in_codes, in_scales, grouped):
+            for j in range(in_codes.shape[1]):
+                acc = psum_p.tile([P, PACK, P], F32)
+                for t in range(PACK):
+                    for g in range(PASSES):
+                        nc.tensor.matmul_mx(
+                            out=acc[:, t, :],
+                            lhsT=w_codes[:, h * PACK + t, g, :].bitcast(FP8X4),
+                            lhsT_scale=w_scales[:, h * PACK + t, g, :],
+                            rhs=in_codes[:, j, g, :].bitcast(FP8X4),
+                            rhs_scale=in_scales[:, j, g, :],
+                            start=(g == 0),
+                            stop=(g == PASSES - 1),
+                        )
+                nc.scalar.copy(out=grouped[:, j * P : (j + 1) * P, :], in_=acc[:].rearrange("p t r -> p r t"))
+
+        q_grouped, q_codes, q_scales = {}, {}, {}
+
+        def project_chunk(c, h):
+            grouped = stage.tile([P, CHUNK_ROWS, PACK], BF16, name="q_grouped", bufs=3, align_bytes=64)
+            q_grouped[c, h] = grouped
+            project(wq_codes, wq_scales, h, x_codes[c], x_scales[c], grouped)
+
+        def quantise_q(c, h):
+            if h == 0:
+                codes = stage.tile([P, PASSES, CHUNK_ROWS], U32, name="q_codes", align_bytes=64)
+                scales = stage.tile([P, PASSES, CHUNK_ROWS], U8, name="q_scales", align_bytes=64)
+                q_codes[c], q_scales[c] = codes, scales
+            nc.vector.quantize_mx(
+                out=q_codes[c][:, h, :].bitcast(FP8X4),
+                scales=q_scales[c][:, h, :],
+                in_=q_grouped[c, h][:].rearrange("p r t -> p (r t)"),
+            )
+
+        logits, shift, expd, total = {}, {}, {}, {}
+
+        def logits_of(c):
+            acc = psum_l.tile([P, CHUNK_SAMPLES, SLOTS], F32, name="logits")
+            logits[c] = acc
+            for h in range(PASSES):
+                nc.tensor.matmul_mx(
+                    out=acc[:].rearrange("p b s -> p (b s)"),
+                    lhsT=k_codes[:, h, :].bitcast(FP8X4),
+                    lhsT_scale=k_scales[:, h, :],
+                    rhs=q_codes[c][:, h, :].bitcast(FP8X4),
+                    rhs_scale=q_scales[c][:, h, :],
+                    start=(h == 0),
+                    stop=(h == PASSES - 1),
+                )
+
+        def row_max(c):
+            top = stage.tile([P, CHUNK_SAMPLES], F32, name="top")
+            nc.vector.reduce_max(out=top[:], in_=logits[c][:], axis=mybir.AxisListType.X)
+            minus = stage.tile([P, CHUNK_SAMPLES], F32, name="minus")
+            nc.vector.tensor_scalar_mul(out=minus[:], in0=top[:], scalar1=-SCALE)
+            shift[c] = minus
+
+        def exponentials(c):
+            e = stage.tile([P, CHUNK_SAMPLES, SLOTS], F32, name="e")
+            s = stage.tile([P, CHUNK_SAMPLES], F32, name="s")
+            expd[c], total[c] = e, s
+            for b in range(CHUNK_SAMPLES):
+                nc.scalar.activation(
+                    out=e[:, b, :],
+                    in_=logits[c][:, b, :],
+                    func=mybir.ActivationFunctionType.Exp,
+                    bias=shift[c][:, b : b + 1],
+                    scale=SCALE,
+                    accum_out=s[:, b : b + 1],
+                )
+
+        def normalise_and_store(c):
+            inverse = stage.tile([P, CHUNK_SAMPLES], F32, name="inverse")
+            nc.vector.reciprocal(out=inverse[:], in_=total[c][:])
+            result = stage.tile([P, CHUNK_SAMPLES, SLOTS], F32, name="result", bufs=3)
+            nc.vector.tensor_tensor(
+                out=result[:],
+                in0=expd[c][:],
+                in1=inverse[:].unsqueeze(2).to_broadcast([P, CHUNK_SAMPLES, SLOTS]),
+                op=mybir.AluOpType.mult,
+            )
+            nc.sync.dma_start(
+                out=out[c * CHUNK_SAMPLES : (c + 1) * CHUNK_SAMPLES, :, :].rearrange("b n s -> n b s"),
+                in_=result[:],
+            )
+
+        wq_codes = keep.tile([P, PASSES * PACK, PASSES, P], U32, align_bytes=64)
+        wq_scales = keep.tile([P, PASSES * PACK, PASSES, P], U8, align_bytes=64)
+        wk_codes = keep.tile([P, PASSES * PACK, PASSES, P], U32, align_bytes=64)
+        wk_scales = keep.tile([P, PASSES * PACK, PASSES, P], U8, align_bytes=64)
+        ident_codes = keep.tile([P, 1, PASSES, P], U32, align_bytes=64)
+        ident_scales = keep.tile([P, 1, PASSES, P], U8, align_bytes=64)
+        k_grouped = keep.tile([P, PASSES, OBJECTS, PACK], BF16, align_bytes=64)
+        k_codes = keep.tile([P, PASSES, OBJECTS], U32, align_bytes=64)
+        k_scales = keep.tile([P, PASSES, OBJECTS], U8, align_bytes=64)
+
+        def prepare_weight_half(raw, codes, scales, h):
+            blocks = slice(h * PACK, (h + 1) * PACK)
+            prepare(raw[h], codes[:, blocks], scales[:, blocks])
+
+        def prepare_chunk(c):
+            new_chunk_codes(c)
+            prepare(x_raw[c], x_codes[c][:], x_scales[c][:])
+
+        prepare_chunk(0)
+        prepare_weight_half(wq_raw, wq_codes, wq_scales, 0)
+        prepare_weight_half(wq_raw, wq_codes, wq_scales, 1)
+        project_chunk(0, 0)
+        prepare_chunk(1)
+        prepare(ident_raw, ident_codes[:], ident_scales[:])
+        prepare_weight_half(wk_raw, wk_codes, wk_scales, 0)
+        project_chunk(0, 1)
+        prepare_weight_half(wk_raw, wk_codes, wk_scales, 1)
+        quantise_q(0, 0)
+        x_grouped[2] = regroup_blocks(transpose_blocks(x_raw[2]), both)
+        for h in range(PASSES):
+            project(wk_codes, wk_scales, h, ident_codes, ident_scales, k_grouped[:, h])
+        nc.vector.quantize_mx(
+            out=k_codes[:].rearrange("p h n -> p (h n)").bitcast(FP8X4),
+            scales=k_scales[:].rearrange("p h n -> p (h n)"),
+            in_=k_grouped[:].rearrange("p h n t -> p (h n t)"),
+        )
+
+        for c in range(1, CHUNKS):
+            quantise_q(c - 1, 1)
+            if c >= 2:
+                normalise_and_store(c - 2)
+            project_chunk(c, 0)
+            logits_of(c - 1)
+            if c + 1 < CHUNKS:
+                quantise_chunk(c + 1)
+            row_max(c - 1)
+            project_chunk(c, 1)
+            quantise_q(c, 0)
+            exponentials(c - 1)
+            if c + 2 < CHUNKS:
+                x_grouped[c + 2] = regroup_blocks(transpose_blocks(x_raw[c + 2]), vector_only)
+
+        last = CHUNKS - 1
+        quantise_q(last, 1)
+        normalise_and_store(last - 1)
+        logits_of(last)
+        row_max(last)
+        exponentials(last)
+        normalise_and_store(last)

@@ -20,7 +20,9 @@ BLOCK_COLS = PASSES * P * PACK
 GROUP = 4
 CHUNK_ROWS = GROUP * P
 CHUNKS = SAMPLES * SLOTS // CHUNK_ROWS
-CHUNK_SAMPLES = CHUNK_ROWS // SLOTS
+BLOCK_SAMPLES = P // SLOTS
+WHOLE = (0, GROUP)
+HALVES = ((0, GROUP // 2), (GROUP // 2, GROUP // 2))
 SCALE = FEATURES ** -0.5
 
 FLOPS = 2 * FEATURES * (SAMPLES * SLOTS * FEATURES + OBJECTS * FEATURES + SAMPLES * SLOTS * OBJECTS)
@@ -33,9 +35,8 @@ def tile_actionbindingattention_pb_t_kernel(tc, slots, ident, Wq, Wk, out):
     with ExitStack() as ctx:
         keep = ctx.enter_context(tc.tile_pool(name="keep", bufs=1))
         stage = ctx.enter_context(tc.tile_pool(name="stage", bufs=2))
-        psum_t = ctx.enter_context(tc.psum_pool(name="psum_t", bufs=GROUP))
+        psum_t = ctx.enter_context(tc.psum_pool(name="psum_t", bufs=GROUP + 1))
         psum_p = ctx.enter_context(tc.psum_pool(name="psum_p", bufs=3))
-        psum_l = ctx.enter_context(tc.psum_pool(name="psum_l", bufs=1))
         ctx.enter_context(tc.manual_schedule())
 
         identity = keep.tile([P, P], F32)
@@ -44,25 +45,26 @@ def tile_actionbindingattention_pb_t_kernel(tc, slots, ident, Wq, Wk, out):
         nc.vector.memset(warm[:], 0.0)
         nc.scalar.activation(out=warm[:], in_=warm[:], func=mybir.ActivationFunctionType.Exp)
 
-        def load_chunk(c):
-            rows = keep.tile([P, GROUP, FEATURES], BF16, name="x_raw%d" % c)
-            nc.sync.dma_start(
-                out=rows[:],
-                in_=slot_rows[c * CHUNK_ROWS : (c + 1) * CHUNK_ROWS, :].rearrange("(j p) d -> p j d", p=P),
-            )
+        def load(view, name, block_by_block):
+            rows = keep.tile([P, GROUP, FEATURES], BF16, name=name)
+            if block_by_block:
+                for j in range(GROUP):
+                    nc.sync.dma_start(out=rows[:, j, :], in_=view[:, j, :])
+            else:
+                nc.sync.dma_start(out=rows[:], in_=view)
             return rows
 
-        def load_weight_half(w, h, name):
-            rows = keep.tile([P, PACK, FEATURES], BF16, name="%s_raw%d" % (name, h))
-            nc.sync.dma_start(
-                out=rows[:],
-                in_=w[h * K_PASS : (h + 1) * K_PASS, :].rearrange("(p t) d -> p t d", t=PACK),
-            )
-            return rows
+        def load_chunk(c, block_by_block=False):
+            view = slot_rows[c * CHUNK_ROWS : (c + 1) * CHUNK_ROWS, :].rearrange("(j p) d -> p j d", p=P)
+            return load(view, "x_raw%d" % c, block_by_block)
+
+        def load_weight_half(w, h, name, block_by_block=False):
+            view = w[h * K_PASS : (h + 1) * K_PASS, :].rearrange("(p t) d -> p t d", t=PACK)
+            return load(view, "%s_raw%d" % (name, h), block_by_block)
 
         x_raw = {}
-        x_raw[0] = load_chunk(0)
-        wq_raw = [load_weight_half(Wq, h, "wq") for h in range(PASSES)]
+        x_raw[0] = load_chunk(0, block_by_block=True)
+        wq_raw = [load_weight_half(Wq, h, "wq", block_by_block=True) for h in range(PASSES)]
         x_raw[1] = load_chunk(1)
         ident_raw = keep.tile([P, 1, FEATURES], BF16)
         nc.sync.dma_start(out=ident_raw[:, 0, :], in_=ident)
@@ -70,26 +72,20 @@ def tile_actionbindingattention_pb_t_kernel(tc, slots, ident, Wq, Wk, out):
         for c in range(2, CHUNKS):
             x_raw[c] = load_chunk(c)
 
-        def transpose_blocks(rows):
-            banks = []
-            for j in range(rows.shape[1]):
-                words = rows[:, j, :].bitcast(F32)
-                bank = psum_t.tile([P, PASSES, PAIRS, P], F32)
-                for g in range(PASSES):
-                    for u in range(PAIRS):
-                        first = (g * PAIRS + u) * P
-                        nc.tensor.transpose(bank[:, g, u, :], words[:, first : first + P], identity[:])
-                banks.append(bank)
-            return banks
+        def transpose_block(block):
+            words = block.bitcast(F32)
+            bank = psum_t.tile([P, PASSES, PAIRS, P], F32, tag="bank")
+            for g in range(PASSES):
+                for u in range(PAIRS):
+                    word = (g * PAIRS + u) * P
+                    nc.tensor.transpose(bank[:, g, u, :], words[:, word : word + P], identity[:])
+            return bank
 
-        def regroup_blocks(banks, copies):
-            grouped = stage.tile([P, GROUP, BLOCK_COLS], BF16, align_bytes=64)
-            for j, bank in enumerate(banks):
-                copies[j % len(copies)](
-                    out=grouped[:, j, :].bitcast(F32).rearrange("p (g r u) -> p g r u", g=PASSES, u=PAIRS),
-                    in_=bank[:].rearrange("p g u r -> p g r u"),
-                )
-            return grouped[:, 0 : len(banks), :]
+        def regroup_block(copy, bank, grouped_block):
+            copy(
+                out=grouped_block.bitcast(F32).rearrange("p (g r u) -> p g r u", g=PASSES, u=PAIRS),
+                in_=bank[:].rearrange("p g u r -> p g r u"),
+            )
 
         def quantise_blocks(grouped, codes, scales):
             nc.vector.quantize_mx(
@@ -98,11 +94,26 @@ def tile_actionbindingattention_pb_t_kernel(tc, slots, ident, Wq, Wk, out):
                 in_=grouped.rearrange("p j k -> p (j k)"),
             )
 
-        both = (nc.vector.tensor_copy, nc.scalar.copy)
-        vector_only = (nc.vector.tensor_copy,)
+        def new_grouped():
+            grouped = stage.tile([P, GROUP, BLOCK_COLS], BF16, align_bytes=64)
+            return grouped
 
         def prepare(rows, codes, scales):
-            quantise_blocks(regroup_blocks(transpose_blocks(rows), both), codes, scales)
+            copies = (nc.vector.tensor_copy, nc.scalar.copy)
+            blocks = rows.shape[1]
+            grouped = new_grouped()
+            for j in range(blocks + 1):
+                if j < blocks:
+                    regroup_block(copies[j % 2], transpose_block(rows[:, j, :]), grouped[:, j, :])
+                if j > 0:
+                    quantise_blocks(grouped[:, j - 1 : j, :], codes[:, j - 1 : j], scales[:, j - 1 : j])
+
+        def transpose_and_regroup(rows):
+            grouped = new_grouped()
+            banks = [transpose_block(rows[:, j, :]) for j in range(GROUP)]
+            for j in range(GROUP):
+                regroup_block(nc.vector.tensor_copy, banks[j], grouped[:, j, :])
+            return grouped
 
         x_grouped, x_codes, x_scales = {}, {}, {}
 
@@ -113,7 +124,7 @@ def tile_actionbindingattention_pb_t_kernel(tc, slots, ident, Wq, Wk, out):
 
         def quantise_chunk(c):
             new_chunk_codes(c)
-            quantise_blocks(x_grouped[c], x_codes[c][:], x_scales[c][:])
+            quantise_blocks(x_grouped[c][:], x_codes[c][:], x_scales[c][:])
 
         def project(w_codes, w_scales, h, in_codes, in_scales, grouped):
             for j in range(in_codes.shape[1]):
@@ -134,70 +145,74 @@ def tile_actionbindingattention_pb_t_kernel(tc, slots, ident, Wq, Wk, out):
         q_grouped, q_codes, q_scales = {}, {}, {}
 
         def project_chunk(c, h):
-            grouped = stage.tile([P, CHUNK_ROWS, PACK], BF16, name="q_grouped", bufs=3, align_bytes=64)
-            q_grouped[c, h] = grouped
-            project(wq_codes, wq_scales, h, x_codes[c], x_scales[c], grouped)
-
-        def quantise_q(c, h):
             if h == 0:
                 codes = stage.tile([P, PASSES, CHUNK_ROWS], U32, name="q_codes", align_bytes=64)
                 scales = stage.tile([P, PASSES, CHUNK_ROWS], U8, name="q_scales", align_bytes=64)
                 q_codes[c], q_scales[c] = codes, scales
+            grouped = stage.tile([P, CHUNK_ROWS, PACK], BF16, name="q_grouped", bufs=3, align_bytes=64)
+            q_grouped[c, h] = grouped
+            project(wq_codes, wq_scales, h, x_codes[c], x_scales[c], grouped)
+
+        def quantise_q(c, h, first, blocks):
+            rows = slice(first * P, (first + blocks) * P)
             nc.vector.quantize_mx(
-                out=q_codes[c][:, h, :].bitcast(FP8X4),
-                scales=q_scales[c][:, h, :],
-                in_=q_grouped[c, h][:].rearrange("p r t -> p (r t)"),
+                out=q_codes[c][:, h, rows].bitcast(FP8X4),
+                scales=q_scales[c][:, h, rows],
+                in_=q_grouped[c, h][:, rows, :].rearrange("p r t -> p (r t)"),
             )
 
         logits, shift, expd, total = {}, {}, {}, {}
 
-        def logits_of(c):
-            acc = psum_l.tile([P, CHUNK_SAMPLES, SLOTS], F32, name="logits")
-            logits[c] = acc
+        def logits_of(c, first, blocks):
+            rows = slice(first * P, (first + blocks) * P)
+            acc = psum_t.tile([P, blocks * BLOCK_SAMPLES, SLOTS], F32, name="logits", tag="bank")
+            logits[c, first] = acc
             for h in range(PASSES):
                 nc.tensor.matmul_mx(
                     out=acc[:].rearrange("p b s -> p (b s)"),
                     lhsT=k_codes[:, h, :].bitcast(FP8X4),
                     lhsT_scale=k_scales[:, h, :],
-                    rhs=q_codes[c][:, h, :].bitcast(FP8X4),
-                    rhs_scale=q_scales[c][:, h, :],
+                    rhs=q_codes[c][:, h, rows].bitcast(FP8X4),
+                    rhs_scale=q_scales[c][:, h, rows],
                     start=(h == 0),
                     stop=(h == PASSES - 1),
                 )
 
-        def row_max(c):
-            top = stage.tile([P, CHUNK_SAMPLES], F32, name="top")
-            nc.vector.reduce_max(out=top[:], in_=logits[c][:], axis=mybir.AxisListType.X)
-            minus = stage.tile([P, CHUNK_SAMPLES], F32, name="minus")
+        def row_max(c, first, blocks):
+            top = stage.tile([P, blocks * BLOCK_SAMPLES], F32, name="top")
+            nc.vector.reduce_max(out=top[:], in_=logits[c, first][:], axis=mybir.AxisListType.X)
+            minus = stage.tile([P, blocks * BLOCK_SAMPLES], F32, name="minus")
             nc.vector.tensor_scalar_mul(out=minus[:], in0=top[:], scalar1=-SCALE)
-            shift[c] = minus
+            shift[c, first] = minus
 
-        def exponentials(c):
-            e = stage.tile([P, CHUNK_SAMPLES, SLOTS], F32, name="e")
-            s = stage.tile([P, CHUNK_SAMPLES], F32, name="s")
-            expd[c], total[c] = e, s
-            for b in range(CHUNK_SAMPLES):
+        def exponentials(c, first, blocks):
+            e = stage.tile([P, blocks * BLOCK_SAMPLES, SLOTS], F32, name="e")
+            s = stage.tile([P, blocks * BLOCK_SAMPLES], F32, name="s")
+            expd[c, first], total[c, first] = e, s
+            for b in range(blocks * BLOCK_SAMPLES):
                 nc.scalar.activation(
                     out=e[:, b, :],
-                    in_=logits[c][:, b, :],
+                    in_=logits[c, first][:, b, :],
                     func=mybir.ActivationFunctionType.Exp,
-                    bias=shift[c][:, b : b + 1],
+                    bias=shift[c, first][:, b : b + 1],
                     scale=SCALE,
                     accum_out=s[:, b : b + 1],
                 )
 
-        def normalise_and_store(c):
-            inverse = stage.tile([P, CHUNK_SAMPLES], F32, name="inverse")
-            nc.vector.reciprocal(out=inverse[:], in_=total[c][:])
-            result = stage.tile([P, CHUNK_SAMPLES, SLOTS], F32, name="result", bufs=3)
+        def normalise_and_store(c, first, blocks):
+            samples = blocks * BLOCK_SAMPLES
+            inverse = stage.tile([P, samples], F32, name="inverse")
+            nc.vector.reciprocal(out=inverse[:], in_=total[c, first][:])
+            result = stage.tile([P, samples, SLOTS], F32, name="result", bufs=3)
             nc.vector.tensor_tensor(
                 out=result[:],
-                in0=expd[c][:],
-                in1=inverse[:].unsqueeze(2).to_broadcast([P, CHUNK_SAMPLES, SLOTS]),
+                in0=expd[c, first][:],
+                in1=inverse[:].unsqueeze(2).to_broadcast([P, samples, SLOTS]),
                 op=mybir.AluOpType.mult,
             )
+            sample = (c * GROUP + first) * BLOCK_SAMPLES
             nc.sync.dma_start(
-                out=out[c * CHUNK_SAMPLES : (c + 1) * CHUNK_SAMPLES, :, :].rearrange("b n s -> n b s"),
+                out=out[sample : sample + samples, :, :].rearrange("b n s -> n b s"),
                 in_=result[:],
             )
 
@@ -228,8 +243,8 @@ def tile_actionbindingattention_pb_t_kernel(tc, slots, ident, Wq, Wk, out):
         prepare_weight_half(wk_raw, wk_codes, wk_scales, 0)
         project_chunk(0, 1)
         prepare_weight_half(wk_raw, wk_codes, wk_scales, 1)
-        quantise_q(0, 0)
-        x_grouped[2] = regroup_blocks(transpose_blocks(x_raw[2]), both)
+        quantise_q(0, 0, *WHOLE)
+        x_grouped[2] = transpose_and_regroup(x_raw[2])
         for h in range(PASSES):
             project(wk_codes, wk_scales, h, ident_codes, ident_scales, k_grouped[:, h])
         nc.vector.quantize_mx(
@@ -239,24 +254,29 @@ def tile_actionbindingattention_pb_t_kernel(tc, slots, ident, Wq, Wk, out):
         )
 
         for c in range(1, CHUNKS):
-            quantise_q(c - 1, 1)
+            quantise_q(c - 1, 1, *WHOLE)
             if c >= 2:
-                normalise_and_store(c - 2)
+                normalise_and_store(c - 2, *WHOLE)
             project_chunk(c, 0)
-            logits_of(c - 1)
+            logits_of(c - 1, *WHOLE)
             if c + 1 < CHUNKS:
                 quantise_chunk(c + 1)
-            row_max(c - 1)
+            row_max(c - 1, *WHOLE)
             project_chunk(c, 1)
-            quantise_q(c, 0)
-            exponentials(c - 1)
+            quantise_q(c, 0, *WHOLE)
+            exponentials(c - 1, *WHOLE)
             if c + 2 < CHUNKS:
-                x_grouped[c + 2] = regroup_blocks(transpose_blocks(x_raw[c + 2]), vector_only)
+                x_grouped[c + 2] = transpose_and_regroup(x_raw[c + 2])
 
         last = CHUNKS - 1
-        quantise_q(last, 1)
-        normalise_and_store(last - 1)
-        logits_of(last)
-        row_max(last)
-        exponentials(last)
-        normalise_and_store(last)
+        for part in HALVES:
+            quantise_q(last, 1, *part)
+        for part in HALVES:
+            logits_of(last, *part)
+        for part in HALVES:
+            row_max(last, *part)
+        normalise_and_store(last - 1, *WHOLE)
+        for part in HALVES:
+            exponentials(last, *part)
+        for part in HALVES:
+            normalise_and_store(last, *part)

@@ -35,8 +35,7 @@ def tile_actionbindingattention_pb_t_kernel(tc, slots, ident, Wq, Wk, out):
     with ExitStack() as ctx:
         keep = ctx.enter_context(tc.tile_pool(name="keep", bufs=1))
         stage = ctx.enter_context(tc.tile_pool(name="stage", bufs=2))
-        psum_t = ctx.enter_context(tc.psum_pool(name="psum_t", bufs=GROUP + 1))
-        psum_p = ctx.enter_context(tc.psum_pool(name="psum_p", bufs=3))
+        psum = ctx.enter_context(tc.psum_pool(name="psum", bufs=8))
         ctx.enter_context(tc.manual_schedule())
 
         identity = keep.tile([P, P], F32)
@@ -74,7 +73,7 @@ def tile_actionbindingattention_pb_t_kernel(tc, slots, ident, Wq, Wk, out):
 
         def transpose_block(block):
             words = block.bitcast(F32)
-            bank = psum_t.tile([P, PASSES, PAIRS, P], F32, tag="bank")
+            bank = psum.tile([P, PASSES, PAIRS, P], F32, tag="bank")
             for g in range(PASSES):
                 for u in range(PAIRS):
                     word = (g * PAIRS + u) * P
@@ -128,7 +127,7 @@ def tile_actionbindingattention_pb_t_kernel(tc, slots, ident, Wq, Wk, out):
 
         def project(w_codes, w_scales, h, in_codes, in_scales, grouped):
             for j in range(in_codes.shape[1]):
-                acc = psum_p.tile([P, PACK, P], F32)
+                acc = psum.tile([P, PACK, P], F32, tag="bank")
                 for t in range(PACK):
                     for g in range(PASSES):
                         nc.tensor.matmul_mx(
@@ -165,7 +164,7 @@ def tile_actionbindingattention_pb_t_kernel(tc, slots, ident, Wq, Wk, out):
 
         def logits_of(c, first, blocks):
             rows = slice(first * P, (first + blocks) * P)
-            acc = psum_t.tile([P, blocks * BLOCK_SAMPLES, SLOTS], F32, name="logits", tag="bank")
+            acc = psum.tile([P, blocks * BLOCK_SAMPLES, SLOTS], F32, name="logits", tag="bank")
             logits[c, first] = acc
             for h in range(PASSES):
                 nc.tensor.matmul_mx(
@@ -186,8 +185,8 @@ def tile_actionbindingattention_pb_t_kernel(tc, slots, ident, Wq, Wk, out):
             shift[c, first] = minus
 
         def exponentials(c, first, blocks):
-            e = stage.tile([P, blocks * BLOCK_SAMPLES, SLOTS], F32, name="e")
-            s = stage.tile([P, blocks * BLOCK_SAMPLES], F32, name="s")
+            e = stage.tile([P, blocks * BLOCK_SAMPLES, SLOTS], F32, name="e", bufs=3)
+            s = stage.tile([P, blocks * BLOCK_SAMPLES], F32, name="s", bufs=3)
             expd[c, first], total[c, first] = e, s
             for b in range(blocks * BLOCK_SAMPLES):
                 nc.scalar.activation(
@@ -254,19 +253,23 @@ def tile_actionbindingattention_pb_t_kernel(tc, slots, ident, Wq, Wk, out):
         )
 
         for c in range(1, CHUNKS):
+            transposes_follow = c + 2 < CHUNKS
             quantise_q(c - 1, 1, *WHOLE)
             if c >= 2:
                 normalise_and_store(c - 2, *WHOLE)
             project_chunk(c, 0)
             logits_of(c - 1, *WHOLE)
+            row_max(c - 1, *WHOLE)
             if c + 1 < CHUNKS:
                 quantise_chunk(c + 1)
-            row_max(c - 1, *WHOLE)
+            if transposes_follow:
+                exponentials(c - 1, *WHOLE)
             project_chunk(c, 1)
             quantise_q(c, 0, *WHOLE)
-            exponentials(c - 1, *WHOLE)
-            if c + 2 < CHUNKS:
+            if transposes_follow:
                 x_grouped[c + 2] = transpose_and_regroup(x_raw[c + 2])
+            else:
+                exponentials(c - 1, *WHOLE)
 
         last = CHUNKS - 1
         for part in HALVES:

@@ -111,7 +111,8 @@ def tile_actionbindingattention_pb_t_kernel(tc, slots, ident, Wq, Wk, out):
             grouped = new_grouped()
             banks = [transpose_block(rows[:, j, :]) for j in range(GROUP)]
             for j in range(GROUP):
-                regroup_block(nc.vector.tensor_copy, banks[j], grouped[:, j, :])
+                copy = nc.scalar.copy if j == GROUP - 1 else nc.vector.tensor_copy
+                regroup_block(copy, banks[j], grouped[:, j, :])
             return grouped
 
         x_grouped, x_codes, x_scales = {}, {}, {}

@@ -22,7 +22,6 @@ CHUNK_ROWS = GROUP * P
 CHUNKS = SAMPLES * SLOTS // CHUNK_ROWS
 BLOCK_SAMPLES = P // SLOTS
 WHOLE = (0, GROUP)
-HALVES = ((0, GROUP // 2), (GROUP // 2, GROUP // 2))
 SCALE = FEATURES ** -0.5
 
 FLOPS = 2 * FEATURES * (SAMPLES * SLOTS * FEATURES + OBJECTS * FEATURES + SAMPLES * SLOTS * OBJECTS)
@@ -31,6 +30,7 @@ FLOPS = 2 * FEATURES * (SAMPLES * SLOTS * FEATURES + OBJECTS * FEATURES + SAMPLE
 def tile_actionbindingattention_pb_t_kernel(tc, slots, ident, Wq, Wk, out):
     nc = tc.nc
     slot_rows = slots.rearrange("b s d -> (b s) d")
+    V, S = nc.vector, nc.scalar
 
     with ExitStack() as ctx:
         keep = ctx.enter_context(tc.tile_pool(name="keep", bufs=1))
@@ -44,34 +44,34 @@ def tile_actionbindingattention_pb_t_kernel(tc, slots, ident, Wq, Wk, out):
         nc.vector.memset(warm[:], 0.0)
         nc.scalar.activation(out=warm[:], in_=warm[:], func=mybir.ActivationFunctionType.Exp)
 
-        def load(view, name, block_by_block):
+        def load(view, name, pieces):
             rows = keep.tile([P, GROUP, FEATURES], BF16, name=name)
-            if block_by_block:
-                for j in range(GROUP):
-                    nc.sync.dma_start(out=rows[:, j, :], in_=view[:, j, :])
-            else:
-                nc.sync.dma_start(out=rows[:], in_=view)
+            step = GROUP // pieces
+            for j in range(0, GROUP, step):
+                nc.sync.dma_start(out=rows[:, j : j + step, :], in_=view[:, j : j + step, :])
             return rows
 
-        def load_chunk(c, block_by_block=False):
+        def load_chunk(c, pieces=1):
             view = slot_rows[c * CHUNK_ROWS : (c + 1) * CHUNK_ROWS, :].rearrange("(j p) d -> p j d", p=P)
-            return load(view, "x_raw%d" % c, block_by_block)
+            return load(view, "x_raw%d" % c, pieces)
 
-        def load_weight_half(w, h, name, block_by_block=False):
+        def load_weight_half(w, h, name, pieces=1):
             view = w[h * K_PASS : (h + 1) * K_PASS, :].rearrange("(p t) d -> p t d", t=PACK)
-            return load(view, "%s_raw%d" % (name, h), block_by_block)
+            return load(view, "%s_raw%d" % (name, h), pieces)
 
-        x_raw = {}
-        x_raw[0] = load_chunk(0, block_by_block=True)
-        wq_raw = [load_weight_half(Wq, h, "wq", block_by_block=True) for h in range(PASSES)]
-        x_raw[1] = load_chunk(1)
+        x_raw, wq_raw, wk_raw = {}, {}, {}
         ident_raw = keep.tile([P, 1, FEATURES], BF16)
+        wq_raw[0] = load_weight_half(Wq, 0, "wq", 4)
+        x_raw[0] = load_chunk(0, 4)
+        wq_raw[1] = load_weight_half(Wq, 1, "wq", 4)
+        x_raw[1] = load_chunk(1, 4)
         nc.sync.dma_start(out=ident_raw[:, 0, :], in_=ident)
-        wk_raw = [load_weight_half(Wk, h, "wk") for h in range(PASSES)]
+        wk_raw[0] = load_weight_half(Wk, 0, "wk")
+        wk_raw[1] = load_weight_half(Wk, 1, "wk")
         for c in range(2, CHUNKS):
             x_raw[c] = load_chunk(c)
 
-        def transpose_block(block):
+        def T(block):
             words = block.bitcast(F32)
             bank = psum.tile([P, PASSES, PAIRS, P], F32, tag="bank")
             for g in range(PASSES):
@@ -80,80 +80,87 @@ def tile_actionbindingattention_pb_t_kernel(tc, slots, ident, Wq, Wk, out):
                     nc.tensor.transpose(bank[:, g, u, :], words[:, word : word + P], identity[:])
             return bank
 
-        def regroup_block(copy, bank, grouped_block):
-            copy(
+        def copy_of(engine):
+            return engine.copy if engine is S else engine.tensor_copy
+
+        def R(engine, bank, grouped_block):
+            copy_of(engine)(
                 out=grouped_block.bitcast(F32).rearrange("p (g r u) -> p g r u", g=PASSES, u=PAIRS),
                 in_=bank[:].rearrange("p g u r -> p g r u"),
             )
 
-        def quantise_blocks(grouped, codes, scales):
+        def Qz(grp, first, blocks):
+            sl = slice(first, first + blocks)
             nc.vector.quantize_mx(
-                out=codes.rearrange("p j g r -> p (j g r)").bitcast(FP8X4),
-                scales=scales.rearrange("p j g r -> p (j g r)"),
-                in_=grouped.rearrange("p j k -> p (j k)"),
+                out=grp["codes"][:, sl].rearrange("p j g r -> p (j g r)").bitcast(FP8X4),
+                scales=grp["scales"][:, sl].rearrange("p j g r -> p (j g r)"),
+                in_=grp["grouped"][:, sl, :].rearrange("p j k -> p (j k)"),
             )
 
-        def new_grouped():
-            grouped = stage.tile([P, GROUP, BLOCK_COLS], BF16, align_bytes=64)
-            return grouped
+        def new_group(raw, codes, scales):
+            grouped = stage.tile([P, GROUP, BLOCK_COLS], BF16, name="grouped", bufs=4, align_bytes=64)
+            return {"raw": raw, "grouped": grouped, "codes": codes, "scales": scales, "banks": {}}
 
-        def prepare(rows, codes, scales):
-            copies = (nc.vector.tensor_copy, nc.scalar.copy)
-            blocks = rows.shape[1]
-            grouped = new_grouped()
-            for j in range(blocks + 1):
-                if j < blocks:
-                    regroup_block(copies[j % 2], transpose_block(rows[:, j, :]), grouped[:, j, :])
-                if j > 0:
-                    quantise_blocks(grouped[:, j - 1 : j, :], codes[:, j - 1 : j], scales[:, j - 1 : j])
+        def Tg(grp, j):
+            grp["banks"][j] = T(grp["raw"][:, j, :])
 
-        def transpose_and_regroup(rows):
-            grouped = new_grouped()
-            banks = [transpose_block(rows[:, j, :]) for j in range(GROUP)]
-            for j in range(GROUP):
-                copy = nc.scalar.copy if j == GROUP - 1 else nc.vector.tensor_copy
-                regroup_block(copy, banks[j], grouped[:, j, :])
-            return grouped
+        def Rg(engine, grp, j):
+            R(engine, grp["banks"][j], grp["grouped"][:, j, :])
 
-        x_grouped, x_codes, x_scales = {}, {}, {}
+        wq_codes = keep.tile([P, PASSES * PACK, PASSES, P], U32, align_bytes=64)
+        wq_scales = keep.tile([P, PASSES * PACK, PASSES, P], U8, align_bytes=64)
+        wk_codes = keep.tile([P, PASSES * PACK, PASSES, P], U32, align_bytes=64)
+        wk_scales = keep.tile([P, PASSES * PACK, PASSES, P], U8, align_bytes=64)
+        ident_codes = keep.tile([P, 1, PASSES, P], U32, align_bytes=64)
+        ident_scales = keep.tile([P, 1, PASSES, P], U8, align_bytes=64)
+        k_grouped = keep.tile([P, PASSES, OBJECTS, PACK], BF16, align_bytes=64)
+        k_codes = keep.tile([P, PASSES, OBJECTS], U32, align_bytes=64)
+        k_scales = keep.tile([P, PASSES, OBJECTS], U8, align_bytes=64)
 
-        def new_chunk_codes(c):
-            codes = stage.tile([P, GROUP, PASSES, P], U32, name="x_codes", align_bytes=64)
-            scales = stage.tile([P, GROUP, PASSES, P], U8, name="x_scales", align_bytes=64)
-            x_codes[c], x_scales[c] = codes, scales
+        def weight_group(raw, codes, scales, h):
+            sl = slice(h * PACK, (h + 1) * PACK)
+            return new_group(raw[h], codes[:, sl], scales[:, sl])
 
-        def quantise_chunk(c):
-            new_chunk_codes(c)
-            quantise_blocks(x_grouped[c][:], x_codes[c][:], x_scales[c][:])
+        xg = {}
 
-        def project(w_codes, w_scales, h, in_codes, in_scales, grouped):
-            for j in range(in_codes.shape[1]):
-                acc = psum.tile([P, PACK, P], F32, tag="bank")
-                for t in range(PACK):
-                    for g in range(PASSES):
-                        nc.tensor.matmul_mx(
-                            out=acc[:, t, :],
-                            lhsT=w_codes[:, h * PACK + t, g, :].bitcast(FP8X4),
-                            lhsT_scale=w_scales[:, h * PACK + t, g, :],
-                            rhs=in_codes[:, j, g, :].bitcast(FP8X4),
-                            rhs_scale=in_scales[:, j, g, :],
-                            start=(g == 0),
-                            stop=(g == PASSES - 1),
-                        )
-                nc.scalar.copy(out=grouped[:, j * P : (j + 1) * P, :], in_=acc[:].rearrange("p t r -> p r t"))
+        def chunk_group(c):
+            codes = stage.tile([P, GROUP, PASSES, P], U32, name="x_codes", bufs=3, align_bytes=64)
+            scales = stage.tile([P, GROUP, PASSES, P], U8, name="x_scales", bufs=3, align_bytes=64)
+            xg[c] = new_group(x_raw[c], codes[:], scales[:])
+            return xg[c]
+
+        def PJ(w_codes, w_scales, h, in_codes, in_scales, j):
+            acc = psum.tile([P, PACK, P], F32, tag="bank")
+            for t in range(PACK):
+                for g in range(PASSES):
+                    nc.tensor.matmul_mx(
+                        out=acc[:, t, :],
+                        lhsT=w_codes[:, h * PACK + t, g, :].bitcast(FP8X4),
+                        lhsT_scale=w_scales[:, h * PACK + t, g, :],
+                        rhs=in_codes[:, j, g, :].bitcast(FP8X4),
+                        rhs_scale=in_scales[:, j, g, :],
+                        start=(g == 0),
+                        stop=(g == PASSES - 1),
+                    )
+            return acc
+
+        def E(engine, acc, grouped_rows):
+            copy_of(engine)(out=grouped_rows, in_=acc[:].rearrange("p t r -> p r t"))
 
         q_grouped, q_codes, q_scales = {}, {}, {}
 
-        def project_chunk(c, h):
-            if h == 0:
-                codes = stage.tile([P, PASSES, CHUNK_ROWS], U32, name="q_codes", align_bytes=64)
-                scales = stage.tile([P, PASSES, CHUNK_ROWS], U8, name="q_scales", align_bytes=64)
+        def PE_(c, h, j, engine):
+            if h == 0 and j == 0:
+                codes = stage.tile([P, PASSES, CHUNK_ROWS], U32, name="q_codes", bufs=3, align_bytes=64)
+                scales = stage.tile([P, PASSES, CHUNK_ROWS], U8, name="q_scales", bufs=3, align_bytes=64)
                 q_codes[c], q_scales[c] = codes, scales
-            grouped = stage.tile([P, CHUNK_ROWS, PACK], BF16, name="q_grouped", bufs=3, align_bytes=64)
-            q_grouped[c, h] = grouped
-            project(wq_codes, wq_scales, h, x_codes[c], x_scales[c], grouped)
+            if j == 0:
+                grouped = stage.tile([P, CHUNK_ROWS, PACK], BF16, name="q_grouped", bufs=4, align_bytes=64)
+                q_grouped[c, h] = grouped
+            acc = PJ(wq_codes, wq_scales, h, xg[c]["codes"], xg[c]["scales"], j)
+            E(engine, acc, q_grouped[c, h][:, j * P : (j + 1) * P, :])
 
-        def quantise_q(c, h, first, blocks):
+        def Qq(c, h, first, blocks):
             rows = slice(first * P, (first + blocks) * P)
             nc.vector.quantize_mx(
                 out=q_codes[c][:, h, rows].bitcast(FP8X4),
@@ -163,7 +170,7 @@ def tile_actionbindingattention_pb_t_kernel(tc, slots, ident, Wq, Wk, out):
 
         logits, shift, expd, total = {}, {}, {}, {}
 
-        def logits_of(c, first, blocks):
+        def L(c, first, blocks):
             rows = slice(first * P, (first + blocks) * P)
             acc = psum.tile([P, blocks * BLOCK_SAMPLES, SLOTS], F32, name="logits", tag="bank")
             logits[c, first] = acc
@@ -178,16 +185,22 @@ def tile_actionbindingattention_pb_t_kernel(tc, slots, ident, Wq, Wk, out):
                     stop=(h == PASSES - 1),
                 )
 
-        def row_max(c, first, blocks):
+        def M(c, first, blocks):
             top = stage.tile([P, blocks * BLOCK_SAMPLES], F32, name="top")
             nc.vector.reduce_max(out=top[:], in_=logits[c, first][:], axis=mybir.AxisListType.X)
+            shift[c, first] = top
+
+        def MUL(c, first, blocks, engine):
             minus = stage.tile([P, blocks * BLOCK_SAMPLES], F32, name="minus")
-            nc.vector.tensor_scalar_mul(out=minus[:], in0=top[:], scalar1=-SCALE)
+            if engine is S:
+                nc.scalar.mul(out=minus[:], in_=shift[c, first][:], mul=-SCALE)
+            else:
+                engine.tensor_scalar_mul(out=minus[:], in0=shift[c, first][:], scalar1=-SCALE)
             shift[c, first] = minus
 
-        def exponentials(c, first, blocks):
-            e = stage.tile([P, blocks * BLOCK_SAMPLES, SLOTS], F32, name="e", bufs=3)
-            s = stage.tile([P, blocks * BLOCK_SAMPLES], F32, name="s", bufs=3)
+        def X(c, first, blocks):
+            e = stage.tile([P, blocks * BLOCK_SAMPLES, SLOTS], F32, name="e", bufs=4)
+            s = stage.tile([P, blocks * BLOCK_SAMPLES], F32, name="s", bufs=4)
             expd[c, first], total[c, first] = e, s
             for b in range(blocks * BLOCK_SAMPLES):
                 nc.scalar.activation(
@@ -199,12 +212,12 @@ def tile_actionbindingattention_pb_t_kernel(tc, slots, ident, Wq, Wk, out):
                     accum_out=s[:, b : b + 1],
                 )
 
-        def normalise_and_store(c, first, blocks):
+        def N(c, first, blocks, engine):
             samples = blocks * BLOCK_SAMPLES
             inverse = stage.tile([P, samples], F32, name="inverse")
             nc.vector.reciprocal(out=inverse[:], in_=total[c, first][:])
             result = stage.tile([P, samples, SLOTS], F32, name="result", bufs=3)
-            nc.vector.tensor_tensor(
+            engine.tensor_tensor(
                 out=result[:],
                 in0=expd[c, first][:],
                 in1=inverse[:].unsqueeze(2).to_broadcast([P, samples, SLOTS]),
@@ -216,71 +229,110 @@ def tile_actionbindingattention_pb_t_kernel(tc, slots, ident, Wq, Wk, out):
                 in_=result[:],
             )
 
-        wq_codes = keep.tile([P, PASSES * PACK, PASSES, P], U32, align_bytes=64)
-        wq_scales = keep.tile([P, PASSES * PACK, PASSES, P], U8, align_bytes=64)
-        wk_codes = keep.tile([P, PASSES * PACK, PASSES, P], U32, align_bytes=64)
-        wk_scales = keep.tile([P, PASSES * PACK, PASSES, P], U8, align_bytes=64)
-        ident_codes = keep.tile([P, 1, PASSES, P], U32, align_bytes=64)
-        ident_scales = keep.tile([P, 1, PASSES, P], U8, align_bytes=64)
-        k_grouped = keep.tile([P, PASSES, OBJECTS, PACK], BF16, align_bytes=64)
-        k_codes = keep.tile([P, PASSES, OBJECTS], U32, align_bytes=64)
-        k_scales = keep.tile([P, PASSES, OBJECTS], U8, align_bytes=64)
 
-        def prepare_weight_half(raw, codes, scales, h):
-            blocks = slice(h * PACK, (h + 1) * PACK)
-            prepare(raw[h], codes[:, blocks], scales[:, blocks])
+        def prep(grp, blocks, engines):
+            for j in range(blocks + 1):
+                if j < blocks:
+                    Tg(grp, j)
+                    Rg(engines[j % len(engines)], grp, j)
+                if j > 0:
+                    Qz(grp, j - 1, 1)
 
-        def prepare_chunk(c):
-            new_chunk_codes(c)
-            prepare(x_raw[c], x_codes[c][:], x_scales[c][:])
+        def kproj():
+            for h in range(PASSES):
+                E(S, PJ(wk_codes, wk_scales, h, ident_codes, ident_scales, 0), k_grouped[:, h])
+            nc.vector.quantize_mx(
+                out=k_codes[:].rearrange("p h n -> p (h n)").bitcast(FP8X4),
+                scales=k_scales[:].rearrange("p h n -> p (h n)"),
+                in_=k_grouped[:].rearrange("p h n t -> p (h n t)"),
+            )
 
-        prepare_chunk(0)
-        prepare_weight_half(wq_raw, wq_codes, wq_scales, 0)
-        prepare_weight_half(wq_raw, wq_codes, wq_scales, 1)
-        project_chunk(0, 0)
-        prepare_chunk(1)
-        prepare(ident_raw, ident_codes[:], ident_scales[:])
-        prepare_weight_half(wk_raw, wk_codes, wk_scales, 0)
-        project_chunk(0, 1)
-        prepare_weight_half(wk_raw, wk_codes, wk_scales, 1)
-        quantise_q(0, 0, *WHOLE)
-        x_grouped[2] = transpose_and_regroup(x_raw[2])
-        for h in range(PASSES):
-            project(wk_codes, wk_scales, h, ident_codes, ident_scales, k_grouped[:, h])
-        nc.vector.quantize_mx(
-            out=k_codes[:].rearrange("p h n -> p (h n)").bitcast(FP8X4),
-            scales=k_scales[:].rearrange("p h n -> p (h n)"),
-            in_=k_grouped[:].rearrange("p h n t -> p (h n t)"),
-        )
+        def run_T(grp, engines):
+            for j in range(GROUP):
+                Tg(grp, j)
+            for j in range(GROUP):
+                Rg(engines[j], grp, j)
 
-        for c in range(1, CHUNKS):
-            transposes_follow = c + 2 < CHUNKS
-            quantise_q(c - 1, 1, *WHOLE)
-            if c >= 2:
-                normalise_and_store(c - 2, *WHOLE)
-            project_chunk(c, 0)
-            logits_of(c - 1, *WHOLE)
-            row_max(c - 1, *WHOLE)
+        ENG = (V, S)
+        prep(weight_group(wq_raw, wq_codes, wq_scales, 0), GROUP, ENG)
+        prep(chunk_group(0), GROUP, ENG)
+        for j in range(GROUP):
+            PE_(0, 0, j, S)
+        prep(weight_group(wq_raw, wq_codes, wq_scales, 1), GROUP, ENG)
+        prep(chunk_group(1), GROUP, ENG)
+        prep(new_group(ident_raw, ident_codes[:], ident_scales[:]), 1, ENG)
+        for j in range(GROUP):
+            PE_(0, 1, j, S)
+        Qq(0, 0, *WHOLE)
+        for j in range(GROUP):
+            PE_(1, 0, j, S)
+        Qq(0, 1, *WHOLE)
+        wk0 = weight_group(wk_raw, wk_codes, wk_scales, 0)
+        wk1 = weight_group(wk_raw, wk_codes, wk_scales, 1)
+        run_T(wk0, (V, V, S, S))
+        run_T(wk1, (V, S, V, S))
+        Qz(wk0, 0, 4)
+        Qz(wk1, 0, 4)
+        for j in range(GROUP):
+            PE_(1, 1, j, S)
+        Qq(1, 0, *WHOLE)
+        g2 = chunk_group(2)
+        g3 = chunk_group(3)
+        for j in range(GROUP):
+            Tg(g2, j)
+        for j in range(GROUP):
+            Tg(g3, j)
+        for j in range(GROUP):
+            Rg((V, S)[j % 2], g2, j)
+        Qz(g2, 0, 4)
+        for j in range(GROUP):
+            Rg((S, V)[j % 2], g3, j)
+        kproj()
+        Qq(1, 1, *WHOLE)
+
+        def soft1(c):
+            L(c, *WHOLE)
+            M(c, *WHOLE)
+            MUL(c, *WHOLE, V)
+
+        for c in range(2, CHUNKS):
+            tf = c + 2 < CHUNKS
+            if c > 2:
+                Qq(c - 1, 1, *WHOLE)
+            if c == 3:
+                N(0, *WHOLE, V)
+            if c >= 4:
+                N(c - 2, *WHOLE, V)
+            for j in range(GROUP):
+                PE_(c, 0, j, S)
+            soft1(0 if c == 2 else c - 1)
             if c + 1 < CHUNKS:
-                quantise_chunk(c + 1)
-            if transposes_follow:
-                exponentials(c - 1, *WHOLE)
-            project_chunk(c, 1)
-            quantise_q(c, 0, *WHOLE)
-            if transposes_follow:
-                x_grouped[c + 2] = transpose_and_regroup(x_raw[c + 2])
+                Qz(xg[c + 1], 0, 4)
+            if tf:
+                X(0 if c == 2 else c - 1, *WHOLE)
+            for j in range(GROUP):
+                PE_(c, 1, j, S)
+            if c == 2:
+                soft1(1)
+                X(1, *WHOLE)
+            if c == 3:
+                N(1, *WHOLE, V)
+            Qq(c, 0, *WHOLE)
+            if tf:
+                run_T(chunk_group(c + 2), (V, V, V, S))
             else:
-                exponentials(c - 1, *WHOLE)
-
+                X(c - 1, *WHOLE)
         last = CHUNKS - 1
+        HALVES = ((0, 2), (2, 2))
         for part in HALVES:
-            quantise_q(last, 1, *part)
+            Qq(last, 1, *part)
         for part in HALVES:
-            logits_of(last, *part)
+            L(last, *part)
         for part in HALVES:
-            row_max(last, *part)
-        normalise_and_store(last - 1, *WHOLE)
+            M(last, *part)
+            MUL(last, *part, V)
+        N(last - 1, *WHOLE, V)
         for part in HALVES:
-            exponentials(last, *part)
+            X(last, *part)
         for part in HALVES:
-            normalise_and_store(last, *part)
+            N(last, *part, V)

@@ -186,12 +186,12 @@ def tile_actionbindingattention_pb_t_kernel(tc, slots, ident, Wq, Wk, out):
                 )
 
         def M(c, first, blocks):
-            top = stage.tile([P, blocks * BLOCK_SAMPLES], F32, name="top")
+            top = stage.tile([P, blocks * BLOCK_SAMPLES], F32, name="top", bufs=4)
             nc.vector.reduce_max(out=top[:], in_=logits[c, first][:], axis=mybir.AxisListType.X)
             shift[c, first] = top
 
         def MUL(c, first, blocks, engine):
-            minus = stage.tile([P, blocks * BLOCK_SAMPLES], F32, name="minus")
+            minus = stage.tile([P, blocks * BLOCK_SAMPLES], F32, name="minus", bufs=4)
             if engine is S:
                 nc.scalar.mul(out=minus[:], in_=shift[c, first][:], mul=-SCALE)
             else:
@@ -212,17 +212,36 @@ def tile_actionbindingattention_pb_t_kernel(tc, slots, ident, Wq, Wk, out):
                     accum_out=s[:, b : b + 1],
                 )
 
-        def N(c, first, blocks, engine):
-            samples = blocks * BLOCK_SAMPLES
-            inverse = stage.tile([P, samples], F32, name="inverse")
+        inv = {}
+
+        def RCP(c, first, blocks):
+            inverse = stage.tile([P, blocks * BLOCK_SAMPLES], F32, name="inverse", bufs=4)
             nc.vector.reciprocal(out=inverse[:], in_=total[c, first][:])
-            result = stage.tile([P, samples, SLOTS], F32, name="result", bufs=3)
-            engine.tensor_tensor(
-                out=result[:],
-                in0=expd[c, first][:],
-                in1=inverse[:].unsqueeze(2).to_broadcast([P, samples, SLOTS]),
-                op=mybir.AluOpType.mult,
-            )
+            inv[c, first] = inverse
+
+        def N(c, first, blocks, engine):
+            RCP(c, first, blocks)
+            NM(c, first, blocks, engine)
+
+        def NM(c, first, blocks, engine):
+            samples = blocks * BLOCK_SAMPLES
+            inverse = inv[c, first]
+            result = stage.tile([P, samples, SLOTS], F32, name="result", bufs=6)
+            if engine is S:
+                for b in range(samples):
+                    nc.scalar.activation(
+                        out=result[:, b, :],
+                        in_=expd[c, first][:, b, :],
+                        func=mybir.ActivationFunctionType.Copy,
+                        scale=inverse[:, b : b + 1],
+                    )
+            else:
+                engine.tensor_tensor(
+                    out=result[:],
+                    in0=expd[c, first][:],
+                    in1=inverse[:].unsqueeze(2).to_broadcast([P, samples, SLOTS]),
+                    op=mybir.AluOpType.mult,
+                )
             sample = (c * GROUP + first) * BLOCK_SAMPLES
             nc.sync.dma_start(
                 out=out[sample : sample + samples, :, :].rearrange("b n s -> n b s"),
@@ -295,8 +314,7 @@ def tile_actionbindingattention_pb_t_kernel(tc, slots, ident, Wq, Wk, out):
             M(c, *WHOLE)
             MUL(c, *WHOLE, V)
 
-        for c in range(2, CHUNKS):
-            tf = c + 2 < CHUNKS
+        for c in range(2, CHUNKS - 2):
             if c > 2:
                 Qq(c - 1, 1, *WHOLE)
             if c == 3:
@@ -306,10 +324,8 @@ def tile_actionbindingattention_pb_t_kernel(tc, slots, ident, Wq, Wk, out):
             for j in range(GROUP):
                 PE_(c, 0, j, S)
             soft1(0 if c == 2 else c - 1)
-            if c + 1 < CHUNKS:
-                Qz(xg[c + 1], 0, 4)
-            if tf:
-                X(0 if c == 2 else c - 1, *WHOLE)
+            Qz(xg[c + 1], 0, 4)
+            X(0 if c == 2 else c - 1, *WHOLE)
             for j in range(GROUP):
                 PE_(c, 1, j, S)
             if c == 2:
@@ -318,21 +334,54 @@ def tile_actionbindingattention_pb_t_kernel(tc, slots, ident, Wq, Wk, out):
             if c == 3:
                 N(1, *WHOLE, V)
             Qq(c, 0, *WHOLE)
-            if tf:
-                run_T(chunk_group(c + 2), (V, V, V, S))
-            else:
-                X(c - 1, *WHOLE)
-        last = CHUNKS - 1
-        HALVES = ((0, 2), (2, 2))
-        for part in HALVES:
-            Qq(last, 1, *part)
-        for part in HALVES:
-            L(last, *part)
-        for part in HALVES:
-            M(last, *part)
-            MUL(last, *part, V)
-        N(last - 1, *WHOLE, V)
-        for part in HALVES:
-            X(last, *part)
-        for part in HALVES:
-            N(last, *part, V)
+            run_T(chunk_group(c + 2), (V, V, V, S))
+
+        Qq(5, 1, *WHOLE)
+        N(4, *WHOLE, V)
+        PE_(6, 0, 0, S)
+        PE_(6, 0, 1, S)
+        PE_(6, 0, 2, V)
+        PE_(6, 0, 3, S)
+        soft1(5)
+        Qz(xg[7], 0, 4)
+        PE_(6, 1, 0, S)
+        X(5, *WHOLE)
+        Qq(6, 0, *WHOLE)
+        PE_(6, 1, 1, V)
+        PE_(6, 1, 2, S)
+        PE_(6, 1, 3, S)
+        Qq(6, 1, *WHOLE)
+        N(5, *WHOLE, V)
+        PE_(7, 0, 0, S)
+        PE_(7, 0, 1, S)
+        PE_(7, 0, 2, S)
+        soft1(6)
+        PE_(7, 0, 3, S)
+        X(6, *WHOLE)
+        PE_(7, 1, 0, V)
+        PE_(7, 1, 1, V)
+        Qq(7, 0, *WHOLE)
+        Qq(7, 1, 0, 2)
+        RCP(6, *WHOLE)
+        PE_(7, 1, 2, S)
+        PE_(7, 1, 3, S)
+        L(7, 0, 2)
+        Qq(7, 1, 2, 1)
+        L(7, 2, 1)
+        M(7, 0, 2)
+        Qq(7, 1, 3, 1)
+        L(7, 3, 1)
+        MUL(7, 0, 2, V)
+        M(7, 2, 1)
+        NM(6, *WHOLE, S)
+        X(7, 0, 2)
+        MUL(7, 2, 1, V)
+        M(7, 3, 1)
+        X(7, 2, 1)
+        MUL(7, 3, 1, V)
+        X(7, 3, 1)
+        N(7, 0, 2, V)
+        RCP(7, 2, 1)
+        RCP(7, 3, 1)
+        NM(7, 2, 1, V)
+        NM(7, 3, 1, V)

@@ -52,7 +52,11 @@ def tile_actionbindingattention_pb_t_kernel(tc, slots, ident, Wq, Wk, out):
             return rows
 
         def load_chunk(c, pieces=1):
-            view = slot_rows[c * CHUNK_ROWS : (c + 1) * CHUNK_ROWS, :].rearrange("(j p) d -> p j d", p=P)
+            rows = slot_rows[c * CHUNK_ROWS : (c + 1) * CHUNK_ROWS, :]
+            if c in DEALT:
+                view = rows.rearrange("(p j) d -> p j d", j=GROUP)
+            else:
+                view = rows.rearrange("(j p) d -> p j d", p=P)
             return load(view, "x_raw%d" % c, pieces)
 
         def load_weight_half(w, h, name, pieces=1):
@@ -60,6 +64,7 @@ def tile_actionbindingattention_pb_t_kernel(tc, slots, ident, Wq, Wk, out):
             return load(view, "%s_raw%d" % (name, h), pieces)
 
         x_raw, wq_raw, wk_raw = {}, {}, {}
+        DEALT = ()
         ident_raw = keep.tile([P, 1, FEATURES], BF16)
         wq_raw[0] = load_weight_half(Wq, 0, "wq", 4)
         x_raw[0] = load_chunk(0, 4)
@@ -187,7 +192,14 @@ def tile_actionbindingattention_pb_t_kernel(tc, slots, ident, Wq, Wk, out):
 
         def M(c, first, blocks):
             top = stage.tile([P, blocks * BLOCK_SAMPLES], F32, name="top", bufs=4)
-            nc.vector.reduce_max(out=top[:], in_=logits[c, first][:], axis=mybir.AxisListType.X)
+            if c in DEALT:
+                nc.vector.reduce_max(
+                    out=top[:],
+                    in_=logits[c, first][:].rearrange("n b s -> n (b s)").rearrange("n (j b i) -> n b j i", j=GROUP, i=SLOTS // GROUP),
+                    axis=mybir.AxisListType.XY,
+                )
+            else:
+                nc.vector.reduce_max(out=top[:], in_=logits[c, first][:], axis=mybir.AxisListType.X)
             shift[c, first] = top
 
         def MUL(c, first, blocks, engine):
@@ -202,10 +214,11 @@ def tile_actionbindingattention_pb_t_kernel(tc, slots, ident, Wq, Wk, out):
             e = stage.tile([P, blocks * BLOCK_SAMPLES, SLOTS], F32, name="e", bufs=4)
             s = stage.tile([P, blocks * BLOCK_SAMPLES], F32, name="s", bufs=4)
             expd[c, first], total[c, first] = e, s
+            dealt = logits[c, first][:].rearrange("n b s -> n (b s)").rearrange("n (j b i) -> n b i j", j=GROUP, i=SLOTS // GROUP) if c in DEALT else None
             for b in range(blocks * BLOCK_SAMPLES):
                 nc.scalar.activation(
-                    out=e[:, b, :],
-                    in_=logits[c, first][:, b, :],
+                    out=e[:, b, :].rearrange("n (i j) -> n i j", j=GROUP) if c in DEALT else e[:, b, :],
+                    in_=dealt[:, b] if c in DEALT else logits[c, first][:, b, :],
                     func=mybir.ActivationFunctionType.Exp,
                     bias=shift[c, first][:, b : b + 1],
                     scale=SCALE,
@@ -322,19 +335,19 @@ def tile_actionbindingattention_pb_t_kernel(tc, slots, ident, Wq, Wk, out):
             if c >= 4:
                 N(c - 2, *WHOLE, V)
             for j in range(GROUP):
-                PE_(c, 0, j, S)
+                PE_(c, 0, j, (S, S, S, S)[j])
             soft1(0 if c == 2 else c - 1)
             Qz(xg[c + 1], 0, 4)
             X(0 if c == 2 else c - 1, *WHOLE)
             for j in range(GROUP):
-                PE_(c, 1, j, S)
+                PE_(c, 1, j, (S, V, S, S)[j])
             if c == 2:
                 soft1(1)
                 X(1, *WHOLE)
             if c == 3:
                 N(1, *WHOLE, V)
             Qq(c, 0, *WHOLE)
-            run_T(chunk_group(c + 2), (V, V, V, S))
+            run_T(chunk_group(c + 2), (V, V, S, S))
 
         Qq(5, 1, *WHOLE)
         N(4, *WHOLE, V)

@@ -71,10 +71,10 @@ def tile_actionbindingattention_pb_t_kernel(tc, slots, ident, Wq, Wk, out):
         wq_raw[1] = load_weight_half(Wq, 1, "wq", 4)
         x_raw[1] = load_chunk(1, 4)
         nc.sync.dma_start(out=ident_raw[:, 0, :], in_=ident)
-        wk_raw[0] = load_weight_half(Wk, 0, "wk")
-        wk_raw[1] = load_weight_half(Wk, 1, "wk")
+        wk_raw[0] = load_weight_half(Wk, 0, "wk", 4)
+        wk_raw[1] = load_weight_half(Wk, 1, "wk", 4)
         for c in range(2, CHUNKS):
-            x_raw[c] = load_chunk(c)
+            x_raw[c] = load_chunk(c, 4 if c < 4 else 1)
 
         def T(block):
             words = block.bitcast(F32)

from contextlib import ExitStack

import concourse.mybir as mybir
from concourse.masks import make_identity

F32 = mybir.dt.float32
BF16 = mybir.dt.bfloat16
U32 = mybir.dt.uint32
U8 = mybir.dt.uint8
FP8X4 = mybir.dt.float8_e4m3fn_x4

P = 128
PACK = 4
K_PASS = P * PACK

SAMPLES, SLOTS, OBJECTS, FEATURES = 64, 64, 128, 1024
PASSES = FEATURES // K_PASS
PAIRS = PACK // 2
BLOCK_COLS = PASSES * P * PACK
GROUP = 4
CHUNK_ROWS = GROUP * P
CHUNKS = SAMPLES * SLOTS // CHUNK_ROWS
BLOCK_SAMPLES = P // SLOTS
WHOLE = (0, GROUP)
SCALE = FEATURES ** -0.5

FLOPS = 2 * FEATURES * (SAMPLES * SLOTS * FEATURES + OBJECTS * FEATURES + SAMPLES * SLOTS * OBJECTS)


def tile_actionbindingattention_pb_t_kernel(tc, slots, ident, Wq, Wk, out):
    nc = tc.nc
    slot_rows = slots.rearrange("b s d -> (b s) d")
    V, S = nc.vector, nc.scalar

    with ExitStack() as ctx:
        keep = ctx.enter_context(tc.tile_pool(name="keep", bufs=1))
        stage = ctx.enter_context(tc.tile_pool(name="stage", bufs=2))
        psum = ctx.enter_context(tc.psum_pool(name="psum", bufs=8))
        ctx.enter_context(tc.manual_schedule())

        identity = keep.tile([P, P], F32)
        make_identity(nc, identity[:])
        warm = keep.tile([P, 1], F32)
        nc.vector.memset(warm[:], 0.0)
        nc.scalar.activation(out=warm[:], in_=warm[:], func=mybir.ActivationFunctionType.Exp)

        def load(view, name, pieces):
            rows = keep.tile([P, GROUP, FEATURES], BF16, name=name)
            step = GROUP // pieces
            for j in range(0, GROUP, step):
                nc.sync.dma_start(out=rows[:, j : j + step, :], in_=view[:, j : j + step, :])
            return rows

        def load_chunk(c, pieces=1):
            rows = slot_rows[c * CHUNK_ROWS : (c + 1) * CHUNK_ROWS, :]
            if c in DEALT:
                view = rows.rearrange("(p j) d -> p j d", j=GROUP)
            else:
                view = rows.rearrange("(j p) d -> p j d", p=P)
            return load(view, "x_raw%d" % c, pieces)

        def load_weight_half(w, h, name, pieces=1):
            view = w[h * K_PASS : (h + 1) * K_PASS, :].rearrange("(p t) d -> p t d", t=PACK)
            return load(view, "%s_raw%d" % (name, h), pieces)

        x_raw, wq_raw, wk_raw = {}, {}, {}
        DEALT = ()
        ident_raw = keep.tile([P, 1, FEATURES], BF16)
        wq_raw[0] = load_weight_half(Wq, 0, "wq", 4)
        x_raw[0] = load_chunk(0, 4)
        wq_raw[1] = load_weight_half(Wq, 1, "wq", 4)
        x_raw[1] = load_chunk(1, 4)
        nc.sync.dma_start(out=ident_raw[:, 0, :], in_=ident)
        wk_raw[0] = load_weight_half(Wk, 0, "wk", 4)
        wk_raw[1] = load_weight_half(Wk, 1, "wk", 4)
        for c in range(2, CHUNKS):
            x_raw[c] = load_chunk(c, 4 if c < 4 else 1)

        def T(block):
            words = block.bitcast(F32)
            bank = psum.tile([P, PASSES, PAIRS, P], F32, tag="bank")
            for g in range(PASSES):
                for u in range(PAIRS):
                    word = (g * PAIRS + u) * P
                    nc.tensor.transpose(bank[:, g, u, :], words[:, word : word + P], identity[:])
            return bank

        def copy_of(engine):
            return engine.copy if engine is S else engine.tensor_copy

        def R(engine, bank, grouped_block):
            copy_of(engine)(
                out=grouped_block.bitcast(F32).rearrange("p (g r u) -> p g r u", g=PASSES, u=PAIRS),
                in_=bank[:].rearrange("p g u r -> p g r u"),
            )

        def Qz(grp, first, blocks):
            sl = slice(first, first + blocks)
            nc.vector.quantize_mx(
                out=grp["codes"][:, sl].rearrange("p j g r -> p (j g r)").bitcast(FP8X4),
                scales=grp["scales"][:, sl].rearrange("p j g r -> p (j g r)"),
                in_=grp["grouped"][:, sl, :].rearrange("p j k -> p (j k)"),
            )

        def new_group(raw, codes, scales):
            grouped = stage.tile([P, GROUP, BLOCK_COLS], BF16, name="grouped", bufs=4, align_bytes=64)
            return {"raw": raw, "grouped": grouped, "codes": codes, "scales": scales, "banks": {}}

        def Tg(grp, j):
            grp["banks"][j] = T(grp["raw"][:, j, :])

        def Rg(engine, grp, j):
            R(engine, grp["banks"][j], grp["grouped"][:, j, :])

        wq_codes = keep.tile([P, PASSES * PACK, PASSES, P], U32, align_bytes=64)
        wq_scales = keep.tile([P, PASSES * PACK, PASSES, P], U8, align_bytes=64)
        wk_codes = keep.tile([P, PASSES * PACK, PASSES, P], U32, align_bytes=64)
        wk_scales = keep.tile([P, PASSES * PACK, PASSES, P], U8, align_bytes=64)
        ident_codes = keep.tile([P, 1, PASSES, P], U32, align_bytes=64)
        ident_scales = keep.tile([P, 1, PASSES, P], U8, align_bytes=64)
        k_grouped = keep.tile([P, PASSES, OBJECTS, PACK], BF16, align_bytes=64)
        k_codes = keep.tile([P, PASSES, OBJECTS], U32, align_bytes=64)
        k_scales = keep.tile([P, PASSES, OBJECTS], U8, align_bytes=64)

        def weight_group(raw, codes, scales, h):
            sl = slice(h * PACK, (h + 1) * PACK)
            return new_group(raw[h], codes[:, sl], scales[:, sl])

        xg = {}

        def chunk_group(c):
            codes = stage.tile([P, GROUP, PASSES, P], U32, name="x_codes", bufs=3, align_bytes=64)
            scales = stage.tile([P, GROUP, PASSES, P], U8, name="x_scales", bufs=3, align_bytes=64)
            xg[c] = new_group(x_raw[c], codes[:], scales[:])
            return xg[c]

        def PJ(w_codes, w_scales, h, in_codes, in_scales, j):
            acc = psum.tile([P, PACK, P], F32, tag="bank")
            for t in range(PACK):
                for g in range(PASSES):
                    nc.tensor.matmul_mx(
                        out=acc[:, t, :],
                        lhsT=w_codes[:, h * PACK + t, g, :].bitcast(FP8X4),
                        lhsT_scale=w_scales[:, h * PACK + t, g, :],
                        rhs=in_codes[:, j, g, :].bitcast(FP8X4),
                        rhs_scale=in_scales[:, j, g, :],
                        start=(g == 0),
                        stop=(g == PASSES - 1),
                    )
            return acc

        def E(engine, acc, grouped_rows):
            copy_of(engine)(out=grouped_rows, in_=acc[:].rearrange("p t r -> p r t"))

        q_grouped, q_codes, q_scales = {}, {}, {}

        def PE_(c, h, j, engine):
            if h == 0 and j == 0:
                codes = stage.tile([P, PASSES, CHUNK_ROWS], U32, name="q_codes", bufs=3, align_bytes=64)
                scales = stage.tile([P, PASSES, CHUNK_ROWS], U8, name="q_scales", bufs=3, align_bytes=64)
                q_codes[c], q_scales[c] = codes, scales
            if j == 0:
                grouped = stage.tile([P, CHUNK_ROWS, PACK], BF16, name="q_grouped", bufs=4, align_bytes=64)
                q_grouped[c, h] = grouped
            acc = PJ(wq_codes, wq_scales, h, xg[c]["codes"], xg[c]["scales"], j)
            E(engine, acc, q_grouped[c, h][:, j * P : (j + 1) * P, :])

        def Qq(c, h, first, blocks):
            rows = slice(first * P, (first + blocks) * P)
            nc.vector.quantize_mx(
                out=q_codes[c][:, h, rows].bitcast(FP8X4),
                scales=q_scales[c][:, h, rows],
                in_=q_grouped[c, h][:, rows, :].rearrange("p r t -> p (r t)"),
            )

        logits, shift, expd, total = {}, {}, {}, {}

        def L(c, first, blocks):
            rows = slice(first * P, (first + blocks) * P)
            acc = psum.tile([P, blocks * BLOCK_SAMPLES, SLOTS], F32, name="logits", tag="bank")
            logits[c, first] = acc
            for h in range(PASSES):
                nc.tensor.matmul_mx(
                    out=acc[:].rearrange("p b s -> p (b s)"),
                    lhsT=k_codes[:, h, :].bitcast(FP8X4),
                    lhsT_scale=k_scales[:, h, :],
                    rhs=q_codes[c][:, h, rows].bitcast(FP8X4),
                    rhs_scale=q_scales[c][:, h, rows],
                    start=(h == 0),
                    stop=(h == PASSES - 1),
                )

        def M(c, first, blocks):
            top = stage.tile([P, blocks * BLOCK_SAMPLES], F32, name="top", bufs=4)
            if c in DEALT:
                nc.vector.reduce_max(
                    out=top[:],
                    in_=logits[c, first][:].rearrange("n b s -> n (b s)").rearrange("n (j b i) -> n b j i", j=GROUP, i=SLOTS // GROUP),
                    axis=mybir.AxisListType.XY,
                )
            else:
                nc.vector.reduce_max(out=top[:], in_=logits[c, first][:], axis=mybir.AxisListType.X)
            shift[c, first] = top

        def MUL(c, first, blocks, engine):
            minus = stage.tile([P, blocks * BLOCK_SAMPLES], F32, name="minus", bufs=4)
            if engine is S:
                nc.scalar.mul(out=minus[:], in_=shift[c, first][:], mul=-SCALE)
            else:
                engine.tensor_scalar_mul(out=minus[:], in0=shift[c, first][:], scalar1=-SCALE)
            shift[c, first] = minus

        def X(c, first, blocks):
            e = stage.tile([P, blocks * BLOCK_SAMPLES, SLOTS], F32, name="e", bufs=4)
            s = stage.tile([P, blocks * BLOCK_SAMPLES], F32, name="s", bufs=4)
            expd[c, first], total[c, first] = e, s
            dealt = logits[c, first][:].rearrange("n b s -> n (b s)").rearrange("n (j b i) -> n b i j", j=GROUP, i=SLOTS // GROUP) if c in DEALT else None
            for b in range(blocks * BLOCK_SAMPLES):
                nc.scalar.activation(
                    out=e[:, b, :].rearrange("n (i j) -> n i j", j=GROUP) if c in DEALT else e[:, b, :],
                    in_=dealt[:, b] if c in DEALT else logits[c, first][:, b, :],
                    func=mybir.ActivationFunctionType.Exp,
                    bias=shift[c, first][:, b : b + 1],
                    scale=SCALE,
                    accum_out=s[:, b : b + 1],
                )

        inv = {}

        def RCP(c, first, blocks):
            inverse = stage.tile([P, blocks * BLOCK_SAMPLES], F32, name="inverse", bufs=4)
            nc.vector.reciprocal(out=inverse[:], in_=total[c, first][:])
            inv[c, first] = inverse

        def N(c, first, blocks, engine):
            RCP(c, first, blocks)
            NM(c, first, blocks, engine)

        def NM(c, first, blocks, engine):
            samples = blocks * BLOCK_SAMPLES
            inverse = inv[c, first]
            result = stage.tile([P, samples, SLOTS], F32, name="result", bufs=6)
            if engine is S:
                for b in range(samples):
                    nc.scalar.activation(
                        out=result[:, b, :],
                        in_=expd[c, first][:, b, :],
                        func=mybir.ActivationFunctionType.Copy,
                        scale=inverse[:, b : b + 1],
                    )
            else:
                engine.tensor_tensor(
                    out=result[:],
                    in0=expd[c, first][:],
                    in1=inverse[:].unsqueeze(2).to_broadcast([P, samples, SLOTS]),
                    op=mybir.AluOpType.mult,
                )
            sample = (c * GROUP + first) * BLOCK_SAMPLES
            nc.sync.dma_start(
                out=out[sample : sample + samples, :, :].rearrange("b n s -> n b s"),
                in_=result[:],
            )


        def prep(grp, blocks, engines):
            for j in range(blocks + 1):
                if j < blocks:
                    Tg(grp, j)
                    Rg(engines[j % len(engines)], grp, j)
                if j > 0:
                    Qz(grp, j - 1, 1)

        def kproj():
            for h in range(PASSES):
                E(S, PJ(wk_codes, wk_scales, h, ident_codes, ident_scales, 0), k_grouped[:, h])
            nc.vector.quantize_mx(
                out=k_codes[:].rearrange("p h n -> p (h n)").bitcast(FP8X4),
                scales=k_scales[:].rearrange("p h n -> p (h n)"),
                in_=k_grouped[:].rearrange("p h n t -> p (h n t)"),
            )

        def run_T(grp, engines):
            for j in range(GROUP):
                Tg(grp, j)
            for j in range(GROUP):
                Rg(engines[j], grp, j)

        ENG = (V, S)
        prep(weight_group(wq_raw, wq_codes, wq_scales, 0), GROUP, ENG)
        prep(chunk_group(0), GROUP, ENG)
        for j in range(GROUP):
            PE_(0, 0, j, S)
        prep(weight_group(wq_raw, wq_codes, wq_scales, 1), GROUP, ENG)
        prep(chunk_group(1), GROUP, ENG)
        prep(new_group(ident_raw, ident_codes[:], ident_scales[:]), 1, ENG)
        for j in range(GROUP):
            PE_(0, 1, j, S)
        Qq(0, 0, *WHOLE)
        for j in range(GROUP):
            PE_(1, 0, j, S)
        Qq(0, 1, *WHOLE)
        wk0 = weight_group(wk_raw, wk_codes, wk_scales, 0)
        wk1 = weight_group(wk_raw, wk_codes, wk_scales, 1)
        run_T(wk0, (V, V, S, S))
        run_T(wk1, (V, S, V, S))
        Qz(wk0, 0, 4)
        Qz(wk1, 0, 4)
        for j in range(GROUP):
            PE_(1, 1, j, S)
        Qq(1, 0, *WHOLE)
        g2 = chunk_group(2)
        g3 = chunk_group(3)
        for j in range(GROUP):
            Tg(g2, j)
        for j in range(GROUP):
            Tg(g3, j)
        for j in range(GROUP):
            Rg((V, S)[j % 2], g2, j)
        Qz(g2, 0, 4)
        for j in range(GROUP):
            Rg((S, V)[j % 2], g3, j)
        kproj()
        Qq(1, 1, *WHOLE)

        def soft1(c):
            L(c, *WHOLE)
            M(c, *WHOLE)
            MUL(c, *WHOLE, V)

        for c in range(2, CHUNKS - 2):
            if c > 2:
                Qq(c - 1, 1, *WHOLE)
            if c == 3:
                N(0, *WHOLE, V)
            if c >= 4:
                N(c - 2, *WHOLE, V)
            for j in range(GROUP):
                PE_(c, 0, j, (S, S, S, S)[j])
            soft1(0 if c == 2 else c - 1)
            Qz(xg[c + 1], 0, 4)
            X(0 if c == 2 else c - 1, *WHOLE)
            for j in range(GROUP):
                PE_(c, 1, j, (S, V, S, S)[j])
            if c == 2:
                soft1(1)
                X(1, *WHOLE)
            if c == 3:
                N(1, *WHOLE, V)
            Qq(c, 0, *WHOLE)
            run_T(chunk_group(c + 2), (V, V, S, S))

        Qq(5, 1, *WHOLE)
        N(4, *WHOLE, V)
        PE_(6, 0, 0, S)
        PE_(6, 0, 1, S)
        PE_(6, 0, 2, V)
        PE_(6, 0, 3, S)
        soft1(5)
        Qz(xg[7], 0, 4)
        PE_(6, 1, 0, S)
        X(5, *WHOLE)
        Qq(6, 0, *WHOLE)
        PE_(6, 1, 1, V)
        PE_(6, 1, 2, S)
        PE_(6, 1, 3, S)
        Qq(6, 1, *WHOLE)
        N(5, *WHOLE, V)
        PE_(7, 0, 0, S)
        PE_(7, 0, 1, S)
        PE_(7, 0, 2, S)
        soft1(6)
        PE_(7, 0, 3, S)
        X(6, *WHOLE)
        PE_(7, 1, 0, V)
        PE_(7, 1, 1, V)
        Qq(7, 0, *WHOLE)
        Qq(7, 1, 0, 2)
        RCP(6, *WHOLE)
        PE_(7, 1, 2, S)
        PE_(7, 1, 3, S)
        L(7, 0, 2)
        Qq(7, 1, 2, 1)
        L(7, 2, 1)
        M(7, 0, 2)
        Qq(7, 1, 3, 1)
        L(7, 3, 1)
        MUL(7, 0, 2, V)
        M(7, 2, 1)
        NM(6, *WHOLE, S)
        X(7, 0, 2)
        MUL(7, 2, 1, V)
        M(7, 3, 1)
        X(7, 2, 1)
        MUL(7, 3, 1, V)
        X(7, 3, 1)
        N(7, 0, 2, V)
        RCP(7, 2, 1)
        RCP(7, 3, 1)
        NM(7, 2, 1, V)
        NM(7, 3, 1, V)
